import numpy as np
import ml_dtypes


def mxq(x, axis, fmt="e4m3"):
    dtype, down = {"e4m3": (ml_dtypes.float8_e4m3fn, 7), "e5m2": (ml_dtypes.float8_e5m2, 14)}[fmt]
    v = np.moveaxis(np.asarray(x, np.float32).astype(ml_dtypes.bfloat16).astype(np.float64), axis, -1)
    blocks = v.reshape(v.shape[:-1] + (-1, 32))
    amax = np.abs(blocks).max(-1, keepdims=True)
    byte = np.maximum(np.where(amax > 0, np.frexp(amax)[1] - 1 + 127, 0) - down, 1)
    scale = np.exp2(byte - 127.0)
    codes = (blocks / scale).astype(np.float32).astype(dtype).astype(np.float64)
    return np.moveaxis((codes * scale).reshape(v.shape), -1, axis)


WIDE = False


def mx_kscale(k):
    if not WIDE:
        return np.ones(k)
    levels = np.array([10, -10, 5, -5, 0])
    a = np.random.permutation(np.resize(levels, k // 512 * 4)).reshape(k // 512, 4)
    idx = np.arange(k)
    return np.exp2(a[idx // 512, idx % 128 // 32])


BF16 = ml_dtypes.bfloat16


def bf(x):
    return np.asarray(x, np.float32).astype(BF16)


def f64(x):
    return np.asarray(x).astype(np.float64)


E, LMAX, MMAX, CIN, COUT = 128, 2, 2, 4096, 128
NS = [LMAX + 1 - m for m in range(MMAX + 1)]
NC = NS[0] + sum(2 * n for n in NS[1:])


def setup_inputs():
    ss = [mx_kscale(n * CIN) for n in NS]
    sx = np.concatenate([ss[0].reshape(NS[0], CIN)] + [np.tile(ss[m].reshape(NS[m], CIN), (2, 1)) for m in range(1, MMAX + 1)], axis=0)
    x = np.random.standard_normal((E, NC, CIN)) * sx
    W0 = np.random.standard_normal((NS[0] * COUT, NS[0] * CIN)) / np.sqrt(NS[0] * CIN) / ss[0][None, :]
    b0 = np.random.standard_normal(NS[0] * COUT) * 0.3
    W1 = np.random.standard_normal((2 * NS[1] * COUT, NS[1] * CIN)) / (np.sqrt(2.0) * np.sqrt(NS[1] * CIN)) / ss[1][None, :]
    W2 = np.random.standard_normal((2 * NS[2] * COUT, NS[2] * CIN)) / (np.sqrt(2.0) * np.sqrt(NS[2] * CIN)) / ss[2][None, :]
    return {"x": bf(x), "W0": bf(W0), "b0": bf(b0), "W1": bf(W1), "W2": bf(W2)}


def reference(x, W0, b0, W1, W2):
    x = f64(x)
    Wm = [f64(W1), f64(W2)]
    outs = []
    x0 = x[:, :LMAX + 1].reshape(E, (LMAX + 1) * CIN)
    y0 = (mxq(x0, 1, "e4m3") @ mxq(f64(W0), 1, "e4m3").T) + f64(b0)
    outs.append(y0.reshape(E, LMAX + 1, COUT))
    offset = LMAX + 1
    for m in range(1, MMAX + 1):
        n = LMAX + 1 - m
        xm = x[:, offset:offset + 2 * n].reshape(E, 2, n * CIN)
        offset += 2 * n
        ym = mxq(xm, 2, "e4m3") @ mxq(Wm[m - 1], 1, "e4m3").T
        of = n * COUT
        x_r, x_i = ym[..., :of], ym[..., of:]
        pos = x_r[:, 0] - x_i[:, 1]
        neg = x_r[:, 1] + x_i[:, 0]
        outs.append(pos.reshape(E, n, COUT))
        outs.append(neg.reshape(E, n, COUT))
    return np.concatenate(outs, axis=1)

@@ -1,0 +1,197 @@
+from contextlib import ExitStack
+
+import concourse.masks as masks
+import concourse.mybir as mybir
+
+F32 = mybir.dt.float32
+BF16 = mybir.dt.bfloat16
+U32 = mybir.dt.uint32
+U8 = mybir.dt.uint8
+FP8X4 = mybir.dt.float8_e4m3fn_x4
+ADD = mybir.AluOpType.add
+SUBTRACT = mybir.AluOpType.subtract
+
+P = 128
+PACK = 4
+K_PASS = P * PACK
+HALVES = 2
+CIN = 4096
+COUT = 128
+BANK_F32 = 512
+PAIR = 2
+
+CHUNK_PASSES = 4
+CHUNK_K = CHUNK_PASSES * K_PASS
+CHUNKS_AHEAD = 3
+MAX_TILES = 6
+RAW_BUFS = (CHUNKS_AHEAD + 1) * MAX_TILES
+TRANSPOSE_BANKS = 6
+VECTOR_COPY_EVERY = 4
+
+FLOPS = 2 * P * (384 * 12288 + 2 * 512 * 8192 + 2 * 256 * 4096)
+
+
+def list_stages(x_flat, W0, W1, W2):
+    def weight_tiles(w, slab):
+        return [w[r : r + P, slab * CIN : (slab + 1) * CIN] for r in range(0, w.shape[0], P)]
+
+    def x_tile(component):
+        return x_flat[:, component * CIN : (component + 1) * CIN]
+
+    return [
+        dict(
+            slabs=[weight_tiles(W0, s) + [x_tile(s)] for s in range(3)],
+            products=[(3, 0, 256), (3, 256, 128)],
+        ),
+        dict(
+            slabs=[weight_tiles(W1, s) + [x_tile(3 + s), x_tile(5 + s)] for s in range(2)],
+            products=[(4, 0, 512), (5, 0, 512)],
+        ),
+        dict(
+            slabs=[weight_tiles(W2, 0) + [x_tile(7), x_tile(8)]],
+            products=[(2, 0, 256), (3, 0, 256)],
+        ),
+    ]
+
+
+def tile_so2linear_k_kernel(tc, x, W0, b0, W1, W2, out):
+    nc = tc.nc
+    out_flat = out.rearrange("e c o -> e (c o)")
+    stages = list_stages(x.rearrange("e c k -> e (c k)"), W0, W1, W2)
+
+    chunks = []
+    for s, stage in enumerate(stages):
+        for slab in stage["slabs"]:
+            for k0 in range(0, CIN, CHUNK_K):
+                chunks.append((s, [view[:, k0 : k0 + CHUNK_K] for view in slab]))
+    first_chunk = [min(c for c, chunk in enumerate(chunks) if chunk[0] == s) for s in range(3)]
+    last_chunk = [max(c for c, chunk in enumerate(chunks) if chunk[0] == s) for s in range(3)]
+
+    with ExitStack() as ctx:
+        const = ctx.enter_context(tc.tile_pool(name="const", bufs=1))
+        raw_pool = ctx.enter_context(tc.tile_pool(name="raw", bufs=RAW_BUFS))
+        grouped_pool = ctx.enter_context(tc.tile_pool(name="grouped", bufs=TRANSPOSE_BANKS))
+        quantised_pool = ctx.enter_context(tc.tile_pool(name="quantised", bufs=3))
+        bank_pool = ctx.enter_context(tc.psum_pool(name="banks", bufs=TRANSPOSE_BANKS))
+        sum_pool = ctx.enter_context(tc.psum_pool(name="sums", bufs=1))
+        ctx.enter_context(tc.manual_schedule())
+
+        identity = const.tile([P, P], F32)
+        masks.make_identity(nc, identity[:])
+        ones = const.tile([P, P], BF16)
+        nc.vector.memset(ones[:], 1.0)
+        bias_rows = const.tile([P, BANK_F32], BF16)
+        nc.vector.memset(bias_rows[:], 0.0)
+        nc.scalar.dma_start(out=bias_rows[0:1, 0 : 3 * COUT], in_=b0.rearrange("(o n) -> o n", o=1))
+        out_sb = const.tile([P, 9 * COUT], F32)
+
+        def load(c):
+            raw_tiles = []
+            for view in chunks[c][1]:
+                raw = raw_pool.tile([P, CHUNK_K], BF16, tag="raw")
+                nc.sync.dma_start(out=raw[:], in_=view)
+                raw_tiles.append(raw)
+            return raw_tiles
+
+        def quantise(grouped, codes, scales):
+            nc.vector.quantize_mx(out=codes.bitcast(FP8X4), scales=scales, in_=grouped[:])
+
+        def multiply(c, codes, scales, sums):
+            s = chunks[c][0]
+            for g in range(CHUNK_PASSES):
+                for acc, (x_index, w0, n) in zip(sums, stages[s]["products"]):
+                    x_cols = slice(x_index * P, (x_index + 1) * P)
+                    nc.tensor.matmul_mx(
+                        out=acc[:],
+                        lhsT=codes[:, g, x_cols].bitcast(FP8X4),
+                        lhsT_scale=scales[:, g, x_cols],
+                        rhs=codes[:, g, w0 : w0 + n].bitcast(FP8X4),
+                        rhs_scale=scales[:, g, w0 : w0 + n],
+                        start=(c == first_chunk[s] and g == 0),
+                        stop=(c == last_chunk[s] and g == CHUNK_PASSES - 1),
+                    )
+
+        def finish_m0(sums):
+            bias_bank = bank_pool.tile([P, BANK_F32], F32, tag="bank")
+            nc.tensor.matmul(out=bias_bank[:], lhsT=ones[:], rhs=bias_rows[:], start=True, stop=True)
+            bias = const.tile([P, 3 * COUT], F32)
+            nc.scalar.copy(out=bias[:], in_=bias_bank[:, 0 : 3 * COUT])
+            nc.vector.tensor_tensor(out=out_sb[:, 0:256], in0=sums[0][:], in1=bias[:, 0:256], op=ADD)
+            nc.vector.tensor_tensor(out=out_sb[:, 256:384], in0=sums[1][:], in1=bias[:, 256:384], op=ADD)
+            nc.sync.dma_start(out=out_flat[:, 0:384], in_=out_sb[:, 0:384])
+
+        def finish_complex(sums, n, col):
+            h = n // 2
+            from_xi = const.tile([P, n], F32, tag="from_xi")
+            nc.scalar.copy(out=from_xi[:], in_=sums[1][:])
+            nc.vector.tensor_tensor(
+                out=out_sb[:, col : col + h], in0=sums[0][:, 0:h], in1=from_xi[:, h:n], op=SUBTRACT
+            )
+            nc.vector.tensor_tensor(
+                out=out_sb[:, col + h : col + n], in0=sums[0][:, h:n], in1=from_xi[:, 0:h], op=ADD
+            )
+            nc.sync.dma_start(out=out_flat[:, col : col + n], in_=out_sb[:, col : col + n])
+
+        def multiply_and_finish(c, codes, scales, sums):
+            multiply(c, codes, scales, sums)
+            s = chunks[c][0]
+            if c == last_chunk[s]:
+                if s == 0:
+                    finish_m0(sums)
+                elif s == 1:
+                    finish_complex(sums, 512, 3 * COUT)
+                else:
+                    finish_complex(sums, 256, 7 * COUT)
+
+        raw_of = {}
+        for c in range(min(CHUNKS_AHEAD, len(chunks))):
+            raw_of[c] = load(c)
+
+        banks_done = 0
+        copied = None
+        transposed = None
+        sums = None
+        for c, (s, views) in enumerate(chunks):
+            if c + CHUNKS_AHEAD < len(chunks):
+                raw_of[c + CHUNKS_AHEAD] = load(c + CHUNKS_AHEAD)
+            words_of = [raw[:].bitcast(F32) for raw in raw_of[c]]
+            columns = len(views) * P
+            codes = quantised_pool.tile([P, CHUNK_PASSES, columns], U32, tag="codes", align_bytes=64)
+            scales = quantised_pool.tile([P, CHUNK_PASSES, columns], U8, tag="scales", align_bytes=64)
+
+            for first in range(0, len(views), PAIR):
+                for g in range(CHUNK_PASSES):
+                    bank = bank_pool.tile([P, BANK_F32], F32, tag="bank")
+                    for t in range(PAIR):
+                        for u in range(HALVES):
+                            word0 = (g * HALVES + u) * P
+                            block = (t * HALVES + u) * P
+                            nc.tensor.transpose(
+                                bank[:, block : block + P],
+                                words_of[first + t][:, word0 : word0 + P],
+                                identity[:],
+                            )
+                    grouped = grouped_pool.tile([P, PAIR * P * PACK], BF16, tag="grouped", align_bytes=64)
+                    copy_out = grouped[:].bitcast(F32).rearrange("p (t r u) -> p t r u", t=PAIR, u=HALVES)
+                    copy_in = bank[:].rearrange("p (t u r) -> p t r u", t=PAIR, u=HALVES)
+                    if banks_done % VECTOR_COPY_EVERY == VECTOR_COPY_EVERY - 1:
+                        nc.vector.tensor_copy(out=copy_out, in_=copy_in)
+                    else:
+                        nc.scalar.copy(out=copy_out, in_=copy_in)
+                    banks_done += 1
+                    if copied is not None:
+                        quantise(*copied)
+                    cols = slice(first * P, (first + PAIR) * P)
+                    copied = (grouped, codes[:, g, cols], scales[:, g, cols])
+
+            if transposed is not None:
+                multiply_and_finish(*transposed)
+            if c == first_chunk[s]:
+                sums = [
+                    sum_pool.tile([P, n], F32, name="sum%d" % i, tag="sum%d" % i)
+                    for i, (x_index, w0, n) in enumerate(stages[s]["products"])
+                ]
+            transposed = (c, codes, scales, sums)
+
+        quantise(*copied)
+        multiply_and_finish(*transposed)

@@ -20,11 +20,10 @@ COUT = 128
 BANK_F32 = 512
 PAIR = 2
 
-CHUNK_PASSES = 4
-CHUNK_K = CHUNK_PASSES * K_PASS
-CHUNKS_AHEAD = 3
-MAX_TILES = 6
-RAW_BUFS = (CHUNKS_AHEAD + 1) * MAX_TILES
+LONG_CHUNK = 8
+SHORT_CHUNK = 4
+PAIRS_AHEAD = 5
+RAW_BUFS = (PAIRS_AHEAD + 1) * PAIR
 TRANSPOSE_BANKS = 6
 VECTOR_COPY_EVERY = 4
 
@@ -59,19 +58,23 @@ def tile_so2linear_k_kernel(tc, x, W0, b0, W1, W2, out):
     out_flat = out.rearrange("e c o -> e (c o)")
     stages = list_stages(x.rearrange("e c k -> e (c k)"), W0, W1, W2)
 
+    slabs = [(s, slab) for s, stage in enumerate(stages) for slab in stage["slabs"]]
     chunks = []
-    for s, stage in enumerate(stages):
-        for slab in stage["slabs"]:
-            for k0 in range(0, CIN, CHUNK_K):
-                chunks.append((s, [view[:, k0 : k0 + CHUNK_K] for view in slab]))
+    for i, (s, slab) in enumerate(slabs):
+        passes = SHORT_CHUNK if i in (0, len(slabs) - 1) else LONG_CHUNK
+        for k0 in range(0, CIN, passes * K_PASS):
+            chunks.append((s, passes, [view[:, k0 : k0 + passes * K_PASS] for view in slab]))
     first_chunk = [min(c for c, chunk in enumerate(chunks) if chunk[0] == s) for s in range(3)]
     last_chunk = [max(c for c, chunk in enumerate(chunks) if chunk[0] == s) for s in range(3)]
+    pair_views = [
+        views[first : first + PAIR] for (s, passes, views) in chunks for first in range(0, len(views), PAIR)
+    ]
 
     with ExitStack() as ctx:
         const = ctx.enter_context(tc.tile_pool(name="const", bufs=1))
         raw_pool = ctx.enter_context(tc.tile_pool(name="raw", bufs=RAW_BUFS))
         grouped_pool = ctx.enter_context(tc.tile_pool(name="grouped", bufs=TRANSPOSE_BANKS))
-        quantised_pool = ctx.enter_context(tc.tile_pool(name="quantised", bufs=3))
+        quantised_pool = ctx.enter_context(tc.tile_pool(name="quantised", bufs=2))
         bank_pool = ctx.enter_context(tc.psum_pool(name="banks", bufs=TRANSPOSE_BANKS))
         sum_pool = ctx.enter_context(tc.psum_pool(name="sums", bufs=1))
         ctx.enter_context(tc.manual_schedule())
@@ -85,31 +88,16 @@ def tile_so2linear_k_kernel(tc, x, W0, b0, W1, W2, out):
         nc.scalar.dma_start(out=bias_rows[0:1, 0 : 3 * COUT], in_=b0.rearrange("(o n) -> o n", o=1))
         out_sb = const.tile([P, 9 * COUT], F32)
 
-        def load(c):
+        def load_pair(j):
             raw_tiles = []
-            for view in chunks[c][1]:
-                raw = raw_pool.tile([P, CHUNK_K], BF16, tag="raw")
+            for view in pair_views[j]:
+                raw = raw_pool.tile([P, view.shape[1]], BF16, tag="raw")
                 nc.sync.dma_start(out=raw[:], in_=view)
                 raw_tiles.append(raw)
             return raw_tiles
 
         def quantise(grouped, codes, scales):
             nc.vector.quantize_mx(out=codes.bitcast(FP8X4), scales=scales, in_=grouped[:])
-
-        def multiply(c, codes, scales, sums):
-            s = chunks[c][0]
-            for g in range(CHUNK_PASSES):
-                for acc, (x_index, w0, n) in zip(sums, stages[s]["products"]):
-                    x_cols = slice(x_index * P, (x_index + 1) * P)
-                    nc.tensor.matmul_mx(
-                        out=acc[:],
-                        lhsT=codes[:, g, x_cols].bitcast(FP8X4),
-                        lhsT_scale=scales[:, g, x_cols],
-                        rhs=codes[:, g, w0 : w0 + n].bitcast(FP8X4),
-                        rhs_scale=scales[:, g, w0 : w0 + n],
-                        start=(c == first_chunk[s] and g == 0),
-                        stop=(c == last_chunk[s] and g == CHUNK_PASSES - 1),
-                    )
 
         def finish_m0(sums):
             bias_bank = bank_pool.tile([P, BANK_F32], F32, tag="bank")
@@ -132,44 +120,63 @@ def tile_so2linear_k_kernel(tc, x, W0, b0, W1, W2, out):
             )
             nc.sync.dma_start(out=out_flat[:, col : col + n], in_=out_sb[:, col : col + n])
 
-        def multiply_and_finish(c, codes, scales, sums):
-            multiply(c, codes, scales, sums)
-            s = chunks[c][0]
-            if c == last_chunk[s]:
+        sums_of = {}
+
+        def multiply(c, codes, scales, g_first, g_count):
+            s, passes = chunks[c][0:2]
+            products = stages[s]["products"]
+            if c == first_chunk[s] and g_first == 0:
+                sums_of[s] = [
+                    sum_pool.tile([P, n], F32, name="sum%d" % i, tag="sum%d" % i)
+                    for i, (x_index, w0, n) in enumerate(products)
+                ]
+            for g in range(g_first, g_first + g_count):
+                for acc, (x_index, w0, n) in zip(sums_of[s], products):
+                    x_cols = slice(x_index * P, (x_index + 1) * P)
+                    nc.tensor.matmul_mx(
+                        out=acc[:],
+                        lhsT=codes[:, g, x_cols].bitcast(FP8X4),
+                        lhsT_scale=scales[:, g, x_cols],
+                        rhs=codes[:, g, w0 : w0 + n].bitcast(FP8X4),
+                        rhs_scale=scales[:, g, w0 : w0 + n],
+                        start=(c == first_chunk[s] and g == 0),
+                        stop=(c == last_chunk[s] and g == passes - 1),
+                    )
+            if c == last_chunk[s] and g_first + g_count == passes:
                 if s == 0:
-                    finish_m0(sums)
+                    finish_m0(sums_of[s])
                 elif s == 1:
-                    finish_complex(sums, 512, 3 * COUT)
+                    finish_complex(sums_of[s], 512, 3 * COUT)
                 else:
-                    finish_complex(sums, 256, 7 * COUT)
+                    finish_complex(sums_of[s], 256, 7 * COUT)
 
         raw_of = {}
-        for c in range(min(CHUNKS_AHEAD, len(chunks))):
-            raw_of[c] = load(c)
+        for j in range(PAIRS_AHEAD):
+            raw_of[j] = load_pair(j)
 
+        j = 0
         banks_done = 0
         copied = None
-        transposed = None
-        sums = None
-        for c, (s, views) in enumerate(chunks):
-            if c + CHUNKS_AHEAD < len(chunks):
-                raw_of[c + CHUNKS_AHEAD] = load(c + CHUNKS_AHEAD)
-            words_of = [raw[:].bitcast(F32) for raw in raw_of[c]]
+        before = None
+        for c, (s, passes, views) in enumerate(chunks):
             columns = len(views) * P
-            codes = quantised_pool.tile([P, CHUNK_PASSES, columns], U32, tag="codes", align_bytes=64)
-            scales = quantised_pool.tile([P, CHUNK_PASSES, columns], U8, tag="scales", align_bytes=64)
+            codes = quantised_pool.tile([P, passes, columns], U32, tag="codes", align_bytes=64)
+            scales = quantised_pool.tile([P, passes, columns], U8, tag="scales", align_bytes=64)
+            gaps = len(views) // PAIR - 1
 
-            for first in range(0, len(views), PAIR):
-                for g in range(CHUNK_PASSES):
+            for pair in range(len(views) // PAIR):
+                if j + PAIRS_AHEAD < len(pair_views):
+                    raw_of[j + PAIRS_AHEAD] = load_pair(j + PAIRS_AHEAD)
+                words_of = [raw[:].bitcast(F32) for raw in raw_of[j]]
+                cols = slice(pair * PAIR * P, (pair + 1) * PAIR * P)
+                for g in range(passes):
                     bank = bank_pool.tile([P, BANK_F32], F32, tag="bank")
                     for t in range(PAIR):
                         for u in range(HALVES):
                             word0 = (g * HALVES + u) * P
                             block = (t * HALVES + u) * P
                             nc.tensor.transpose(
-                                bank[:, block : block + P],
-                                words_of[first + t][:, word0 : word0 + P],
-                                identity[:],
+                                bank[:, block : block + P], words_of[t][:, word0 : word0 + P], identity[:]
                             )
                     grouped = grouped_pool.tile([P, PAIR * P * PACK], BF16, tag="grouped", align_bytes=64)
                     copy_out = grouped[:].bitcast(F32).rearrange("p (t r u) -> p t r u", t=PAIR, u=HALVES)
@@ -181,17 +188,12 @@ def tile_so2linear_k_kernel(tc, x, W0, b0, W1, W2, out):
                     banks_done += 1
                     if copied is not None:
                         quantise(*copied)
-                    cols = slice(first * P, (first + PAIR) * P)
                     copied = (grouped, codes[:, g, cols], scales[:, g, cols])
-
-            if transposed is not None:
-                multiply_and_finish(*transposed)
-            if c == first_chunk[s]:
-                sums = [
-                    sum_pool.tile([P, n], F32, name="sum%d" % i, tag="sum%d" % i)
-                    for i, (x_index, w0, n) in enumerate(stages[s]["products"])
-                ]
-            transposed = (c, codes, scales, sums)
+                j += 1
+                if before is not None and pair < gaps:
+                    share = chunks[before[0]][1] // gaps
+                    multiply(*before, pair * share, share)
+            before = (c, codes, scales)
 
         quantise(*copied)
-        multiply_and_finish(*transposed)
+        multiply(*before, 0, chunks[before[0]][1])

@@ -18,12 +18,12 @@ HALVES = 2
 CIN = 4096
 COUT = 128
 BANK_F32 = 512
-PAIR = 2
+BANK_PASSES = BANK_F32 // (HALVES * P)
 
-LONG_CHUNK = 8
-SHORT_CHUNK = 4
-PAIRS_AHEAD = 5
-RAW_BUFS = (PAIRS_AHEAD + 1) * PAIR
+CHUNK_PASSES = 4
+CHUNK_K = CHUNK_PASSES * K_PASS
+RUN_PASSES = 2
+TILES_AHEAD = 18
 TRANSPOSE_BANKS = 6
 VECTOR_COPY_EVERY = 4
 
@@ -39,16 +39,19 @@ def list_stages(x_flat, W0, W1, W2):
 
     return [
         dict(
-            slabs=[weight_tiles(W0, s) + [x_tile(s)] for s in range(3)],
-            products=[(3, 0, 256), (3, 256, 128)],
-        ),
-        dict(
             slabs=[weight_tiles(W1, s) + [x_tile(3 + s), x_tile(5 + s)] for s in range(2)],
             products=[(4, 0, 512), (5, 0, 512)],
+            out_col=3 * COUT,
+        ),
+        dict(
+            slabs=[weight_tiles(W0, s) + [x_tile(s)] for s in range(3)],
+            products=[(3, 0, 256), (3, 256, 128)],
+            out_col=0,
         ),
         dict(
             slabs=[weight_tiles(W2, 0) + [x_tile(7), x_tile(8)]],
             products=[(2, 0, 256), (3, 0, 256)],
+            out_col=7 * COUT,
         ),
     ]
 
@@ -58,21 +61,18 @@ def tile_so2linear_k_kernel(tc, x, W0, b0, W1, W2, out):
     out_flat = out.rearrange("e c o -> e (c o)")
     stages = list_stages(x.rearrange("e c k -> e (c k)"), W0, W1, W2)
 
-    slabs = [(s, slab) for s, stage in enumerate(stages) for slab in stage["slabs"]]
     chunks = []
-    for i, (s, slab) in enumerate(slabs):
-        passes = SHORT_CHUNK if i in (0, len(slabs) - 1) else LONG_CHUNK
-        for k0 in range(0, CIN, passes * K_PASS):
-            chunks.append((s, passes, [view[:, k0 : k0 + passes * K_PASS] for view in slab]))
-    first_chunk = [min(c for c, chunk in enumerate(chunks) if chunk[0] == s) for s in range(3)]
-    last_chunk = [max(c for c, chunk in enumerate(chunks) if chunk[0] == s) for s in range(3)]
-    pair_views = [
-        views[first : first + PAIR] for (s, passes, views) in chunks for first in range(0, len(views), PAIR)
-    ]
+    for s, stage in enumerate(stages):
+        for slab in stage["slabs"]:
+            for k0 in range(0, CIN, CHUNK_K):
+                chunks.append((s, [view[:, k0 : k0 + CHUNK_K] for view in slab]))
+    first_chunk = [min(c for c, chunk in enumerate(chunks) if chunk[0] == s) for s in range(len(stages))]
+    last_chunk = [max(c for c, chunk in enumerate(chunks) if chunk[0] == s) for s in range(len(stages))]
+    tile_views = [view for (s, views) in chunks for view in views]
 
     with ExitStack() as ctx:
         const = ctx.enter_context(tc.tile_pool(name="const", bufs=1))
-        raw_pool = ctx.enter_context(tc.tile_pool(name="raw", bufs=RAW_BUFS))
+        raw_pool = ctx.enter_context(tc.tile_pool(name="raw", bufs=TILES_AHEAD + 1))
         grouped_pool = ctx.enter_context(tc.tile_pool(name="grouped", bufs=TRANSPOSE_BANKS))
         quantised_pool = ctx.enter_context(tc.tile_pool(name="quantised", bufs=2))
         bank_pool = ctx.enter_context(tc.psum_pool(name="banks", bufs=TRANSPOSE_BANKS))
@@ -88,51 +88,55 @@ def tile_so2linear_k_kernel(tc, x, W0, b0, W1, W2, out):
         nc.scalar.dma_start(out=bias_rows[0:1, 0 : 3 * COUT], in_=b0.rearrange("(o n) -> o n", o=1))
         out_sb = const.tile([P, 9 * COUT], F32)
 
-        def load_pair(j):
-            raw_tiles = []
-            for view in pair_views[j]:
-                raw = raw_pool.tile([P, view.shape[1]], BF16, tag="raw")
-                nc.sync.dma_start(out=raw[:], in_=view)
-                raw_tiles.append(raw)
-            return raw_tiles
+        def load(j):
+            raw = raw_pool.tile([P, CHUNK_K], BF16, tag="raw")
+            nc.sync.dma_start(out=raw[:], in_=tile_views[j])
+            return raw
 
-        def quantise(grouped, codes, scales):
-            nc.vector.quantize_mx(out=codes.bitcast(FP8X4), scales=scales, in_=grouped[:])
+        def quantise(grouped, codes, scales, g0, cols):
+            for i in range(BANK_PASSES):
+                nc.vector.quantize_mx(
+                    out=codes[:, g0 + i, cols].bitcast(FP8X4),
+                    scales=scales[:, g0 + i, cols],
+                    in_=grouped[:, i * K_PASS : (i + 1) * K_PASS],
+                )
 
-        def finish_m0(sums):
+        def finish_with_bias(sums, col):
             bias_bank = bank_pool.tile([P, BANK_F32], F32, tag="bank")
             nc.tensor.matmul(out=bias_bank[:], lhsT=ones[:], rhs=bias_rows[:], start=True, stop=True)
             bias = const.tile([P, 3 * COUT], F32)
             nc.scalar.copy(out=bias[:], in_=bias_bank[:, 0 : 3 * COUT])
-            nc.vector.tensor_tensor(out=out_sb[:, 0:256], in0=sums[0][:], in1=bias[:, 0:256], op=ADD)
-            nc.vector.tensor_tensor(out=out_sb[:, 256:384], in0=sums[1][:], in1=bias[:, 256:384], op=ADD)
-            nc.sync.dma_start(out=out_flat[:, 0:384], in_=out_sb[:, 0:384])
+            nc.vector.tensor_tensor(out=out_sb[:, col : col + 256], in0=sums[0][:], in1=bias[:, 0:256], op=ADD)
+            nc.vector.tensor_tensor(
+                out=out_sb[:, col + 256 : col + 384], in0=sums[1][:], in1=bias[:, 256:384], op=ADD
+            )
+            nc.sync.dma_start(out=out_flat[:, col : col + 384], in_=out_sb[:, col : col + 384])
 
         def finish_complex(sums, n, col):
             h = n // 2
-            from_xi = const.tile([P, n], F32, tag="from_xi")
-            nc.scalar.copy(out=from_xi[:], in_=sums[1][:])
+            from_xr = const.tile([P, n], F32, tag="from_xr")
+            nc.scalar.copy(out=from_xr[:], in_=sums[0][:])
             nc.vector.tensor_tensor(
-                out=out_sb[:, col : col + h], in0=sums[0][:, 0:h], in1=from_xi[:, h:n], op=SUBTRACT
+                out=out_sb[:, col : col + h], in0=from_xr[:, 0:h], in1=sums[1][:, h:n], op=SUBTRACT
             )
             nc.vector.tensor_tensor(
-                out=out_sb[:, col + h : col + n], in0=sums[0][:, h:n], in1=from_xi[:, 0:h], op=ADD
+                out=out_sb[:, col + h : col + n], in0=from_xr[:, h:n], in1=sums[1][:, 0:h], op=ADD
             )
             nc.sync.dma_start(out=out_flat[:, col : col + n], in_=out_sb[:, col : col + n])
 
         sums_of = {}
 
         def multiply(c, codes, scales, g_first, g_count):
-            s, passes = chunks[c][0:2]
+            s = chunks[c][0]
             products = stages[s]["products"]
             if c == first_chunk[s] and g_first == 0:
                 sums_of[s] = [
                     sum_pool.tile([P, n], F32, name="sum%d" % i, tag="sum%d" % i)
                     for i, (x_index, w0, n) in enumerate(products)
                 ]
-            for g in range(g_first, g_first + g_count):
-                for acc, (x_index, w0, n) in zip(sums_of[s], products):
-                    x_cols = slice(x_index * P, (x_index + 1) * P)
+            for acc, (x_index, w0, n) in zip(sums_of[s], products):
+                x_cols = slice(x_index * P, (x_index + 1) * P)
+                for g in range(g_first, g_first + g_count):
                     nc.tensor.matmul_mx(
                         out=acc[:],
                         lhsT=codes[:, g, x_cols].bitcast(FP8X4),
@@ -140,47 +144,42 @@ def tile_so2linear_k_kernel(tc, x, W0, b0, W1, W2, out):
                         rhs=codes[:, g, w0 : w0 + n].bitcast(FP8X4),
                         rhs_scale=scales[:, g, w0 : w0 + n],
                         start=(c == first_chunk[s] and g == 0),
-                        stop=(c == last_chunk[s] and g == passes - 1),
+                        stop=(c == last_chunk[s] and g == CHUNK_PASSES - 1),
                     )
-            if c == last_chunk[s] and g_first + g_count == passes:
-                if s == 0:
-                    finish_m0(sums_of[s])
-                elif s == 1:
-                    finish_complex(sums_of[s], 512, 3 * COUT)
+            if c == last_chunk[s] and g_first + g_count == CHUNK_PASSES:
+                if stages[s]["out_col"] == 0:
+                    finish_with_bias(sums_of[s], 0)
                 else:
-                    finish_complex(sums_of[s], 256, 7 * COUT)
+                    finish_complex(sums_of[s], products[0][2], stages[s]["out_col"])
 
         raw_of = {}
-        for j in range(PAIRS_AHEAD):
-            raw_of[j] = load_pair(j)
+        for j in range(TILES_AHEAD):
+            raw_of[j] = load(j)
 
         j = 0
         banks_done = 0
         copied = None
         before = None
-        for c, (s, passes, views) in enumerate(chunks):
+        for c, (s, views) in enumerate(chunks):
             columns = len(views) * P
-            codes = quantised_pool.tile([P, passes, columns], U32, tag="codes", align_bytes=64)
-            scales = quantised_pool.tile([P, passes, columns], U8, tag="scales", align_bytes=64)
-            gaps = len(views) // PAIR - 1
+            codes = quantised_pool.tile([P, CHUNK_PASSES, columns], U32, tag="codes", align_bytes=64)
+            scales = quantised_pool.tile([P, CHUNK_PASSES, columns], U8, tag="scales", align_bytes=64)
+            run_banks = len(views) * RUN_PASSES // BANK_PASSES
+            banks_in_chunk = 0
 
-            for pair in range(len(views) // PAIR):
-                if j + PAIRS_AHEAD < len(pair_views):
-                    raw_of[j + PAIRS_AHEAD] = load_pair(j + PAIRS_AHEAD)
-                words_of = [raw[:].bitcast(F32) for raw in raw_of[j]]
-                cols = slice(pair * PAIR * P, (pair + 1) * PAIR * P)
-                for g in range(passes):
+            for t in range(len(views)):
+                if j + TILES_AHEAD < len(tile_views):
+                    raw_of[j + TILES_AHEAD] = load(j + TILES_AHEAD)
+                words = raw_of[j][:].bitcast(F32)
+                j += 1
+                for g0 in range(0, CHUNK_PASSES, BANK_PASSES):
                     bank = bank_pool.tile([P, BANK_F32], F32, tag="bank")
-                    for t in range(PAIR):
-                        for u in range(HALVES):
-                            word0 = (g * HALVES + u) * P
-                            block = (t * HALVES + u) * P
-                            nc.tensor.transpose(
-                                bank[:, block : block + P], words_of[t][:, word0 : word0 + P], identity[:]
-                            )
-                    grouped = grouped_pool.tile([P, PAIR * P * PACK], BF16, tag="grouped", align_bytes=64)
-                    copy_out = grouped[:].bitcast(F32).rearrange("p (t r u) -> p t r u", t=PAIR, u=HALVES)
-                    copy_in = bank[:].rearrange("p (t u r) -> p t r u", t=PAIR, u=HALVES)
+                    for b in range(BANK_PASSES * HALVES):
+                        word0 = (g0 * HALVES + b) * P
+                        nc.tensor.transpose(bank[:, b * P : (b + 1) * P], words[:, word0 : word0 + P], identity[:])
+                    grouped = grouped_pool.tile([P, BANK_PASSES * K_PASS], BF16, tag="grouped", align_bytes=64)
+                    copy_out = grouped[:].bitcast(F32).rearrange("p (i r u) -> p i r u", i=BANK_PASSES, u=HALVES)
+                    copy_in = bank[:].rearrange("p (i u r) -> p i r u", i=BANK_PASSES, u=HALVES)
                     if banks_done % VECTOR_COPY_EVERY == VECTOR_COPY_EVERY - 1:
                         nc.vector.tensor_copy(out=copy_out, in_=copy_in)
                     else:
@@ -188,12 +187,12 @@ def tile_so2linear_k_kernel(tc, x, W0, b0, W1, W2, out):
                     banks_done += 1
                     if copied is not None:
                         quantise(*copied)
-                    copied = (grouped, codes[:, g, cols], scales[:, g, cols])
-                j += 1
-                if before is not None and pair < gaps:
-                    share = chunks[before[0]][1] // gaps
-                    multiply(*before, pair * share, share)
+                    copied = (grouped, codes, scales, g0, slice(t * P, (t + 1) * P))
+
+                    banks_in_chunk += 1
+                    if before is not None and banks_in_chunk % run_banks == 0:
+                        multiply(*before, (banks_in_chunk // run_banks - 1) * RUN_PASSES, RUN_PASSES)
             before = (c, codes, scales)
 
         quantise(*copied)
-        multiply(*before, 0, chunks[before[0]][1])
+        multiply(*before, 0, CHUNK_PASSES)

@@ -22,7 +22,7 @@ BANK_PASSES = BANK_F32 // (HALVES * P)
 
 CHUNK_PASSES = 4
 CHUNK_K = CHUNK_PASSES * K_PASS
-RUN_PASSES = 2
+RUN_PASSES = 4
 TILES_AHEAD = 18
 TRANSPOSE_BANKS = 6
 VECTOR_COPY_EVERY = 4

from contextlib import ExitStack

import concourse.masks as masks
import concourse.mybir as mybir

F32 = mybir.dt.float32
BF16 = mybir.dt.bfloat16
U32 = mybir.dt.uint32
U8 = mybir.dt.uint8
FP8X4 = mybir.dt.float8_e4m3fn_x4
ADD = mybir.AluOpType.add
SUBTRACT = mybir.AluOpType.subtract

P = 128
PACK = 4
K_PASS = P * PACK
HALVES = 2
CIN = 4096
COUT = 128
BANK_F32 = 512
BANK_PASSES = BANK_F32 // (HALVES * P)

CHUNK_PASSES = 4
CHUNK_K = CHUNK_PASSES * K_PASS
RUN_PASSES = 4
TILES_AHEAD = 18
TRANSPOSE_BANKS = 6
VECTOR_COPY_EVERY = 4

FLOPS = 2 * P * (384 * 12288 + 2 * 512 * 8192 + 2 * 256 * 4096)


def list_stages(x_flat, W0, W1, W2):
    def weight_tiles(w, slab):
        return [w[r : r + P, slab * CIN : (slab + 1) * CIN] for r in range(0, w.shape[0], P)]

    def x_tile(component):
        return x_flat[:, component * CIN : (component + 1) * CIN]

    return [
        dict(
            slabs=[weight_tiles(W1, s) + [x_tile(3 + s), x_tile(5 + s)] for s in range(2)],
            products=[(4, 0, 512), (5, 0, 512)],
            out_col=3 * COUT,
        ),
        dict(
            slabs=[weight_tiles(W0, s) + [x_tile(s)] for s in range(3)],
            products=[(3, 0, 256), (3, 256, 128)],
            out_col=0,
        ),
        dict(
            slabs=[weight_tiles(W2, 0) + [x_tile(7), x_tile(8)]],
            products=[(2, 0, 256), (3, 0, 256)],
            out_col=7 * COUT,
        ),
    ]


def tile_so2linear_k_kernel(tc, x, W0, b0, W1, W2, out):
    nc = tc.nc
    out_flat = out.rearrange("e c o -> e (c o)")
    stages = list_stages(x.rearrange("e c k -> e (c k)"), W0, W1, W2)

    chunks = []
    for s, stage in enumerate(stages):
        for slab in stage["slabs"]:
            for k0 in range(0, CIN, CHUNK_K):
                chunks.append((s, [view[:, k0 : k0 + CHUNK_K] for view in slab]))
    first_chunk = [min(c for c, chunk in enumerate(chunks) if chunk[0] == s) for s in range(len(stages))]
    last_chunk = [max(c for c, chunk in enumerate(chunks) if chunk[0] == s) for s in range(len(stages))]
    tile_views = [view for (s, views) in chunks for view in views]

    with ExitStack() as ctx:
        const = ctx.enter_context(tc.tile_pool(name="const", bufs=1))
        raw_pool = ctx.enter_context(tc.tile_pool(name="raw", bufs=TILES_AHEAD + 1))
        grouped_pool = ctx.enter_context(tc.tile_pool(name="grouped", bufs=TRANSPOSE_BANKS))
        quantised_pool = ctx.enter_context(tc.tile_pool(name="quantised", bufs=2))
        bank_pool = ctx.enter_context(tc.psum_pool(name="banks", bufs=TRANSPOSE_BANKS))
        sum_pool = ctx.enter_context(tc.psum_pool(name="sums", bufs=1))
        ctx.enter_context(tc.manual_schedule())

        identity = const.tile([P, P], F32)
        masks.make_identity(nc, identity[:])
        ones = const.tile([P, P], BF16)
        nc.vector.memset(ones[:], 1.0)
        bias_rows = const.tile([P, BANK_F32], BF16)
        nc.vector.memset(bias_rows[:], 0.0)
        nc.scalar.dma_start(out=bias_rows[0:1, 0 : 3 * COUT], in_=b0.rearrange("(o n) -> o n", o=1))
        out_sb = const.tile([P, 9 * COUT], F32)

        def load(j):
            raw = raw_pool.tile([P, CHUNK_K], BF16, tag="raw")
            nc.sync.dma_start(out=raw[:], in_=tile_views[j])
            return raw

        def quantise(grouped, codes, scales, g0, cols):
            for i in range(BANK_PASSES):
                nc.vector.quantize_mx(
                    out=codes[:, g0 + i, cols].bitcast(FP8X4),
                    scales=scales[:, g0 + i, cols],
                    in_=grouped[:, i * K_PASS : (i + 1) * K_PASS],
                )

        def finish_with_bias(sums, col):
            bias_bank = bank_pool.tile([P, BANK_F32], F32, tag="bank")
            nc.tensor.matmul(out=bias_bank[:], lhsT=ones[:], rhs=bias_rows[:], start=True, stop=True)
            bias = const.tile([P, 3 * COUT], F32)
            nc.scalar.copy(out=bias[:], in_=bias_bank[:, 0 : 3 * COUT])
            nc.vector.tensor_tensor(out=out_sb[:, col : col + 256], in0=sums[0][:], in1=bias[:, 0:256], op=ADD)
            nc.vector.tensor_tensor(
                out=out_sb[:, col + 256 : col + 384], in0=sums[1][:], in1=bias[:, 256:384], op=ADD
            )
            nc.sync.dma_start(out=out_flat[:, col : col + 384], in_=out_sb[:, col : col + 384])

        def finish_complex(sums, n, col):
            h = n // 2
            from_xr = const.tile([P, n], F32, tag="from_xr")
            nc.scalar.copy(out=from_xr[:], in_=sums[0][:])
            nc.vector.tensor_tensor(
                out=out_sb[:, col : col + h], in0=from_xr[:, 0:h], in1=sums[1][:, h:n], op=SUBTRACT
            )
            nc.vector.tensor_tensor(
                out=out_sb[:, col + h : col + n], in0=from_xr[:, h:n], in1=sums[1][:, 0:h], op=ADD
            )
            nc.sync.dma_start(out=out_flat[:, col : col + n], in_=out_sb[:, col : col + n])

        sums_of = {}

        def multiply(c, codes, scales, g_first, g_count):
            s = chunks[c][0]
            products = stages[s]["products"]
            if c == first_chunk[s] and g_first == 0:
                sums_of[s] = [
                    sum_pool.tile([P, n], F32, name="sum%d" % i, tag="sum%d" % i)
                    for i, (x_index, w0, n) in enumerate(products)
                ]
            for acc, (x_index, w0, n) in zip(sums_of[s], products):
                x_cols = slice(x_index * P, (x_index + 1) * P)
                for g in range(g_first, g_first + g_count):
                    nc.tensor.matmul_mx(
                        out=acc[:],
                        lhsT=codes[:, g, x_cols].bitcast(FP8X4),
                        lhsT_scale=scales[:, g, x_cols],
                        rhs=codes[:, g, w0 : w0 + n].bitcast(FP8X4),
                        rhs_scale=scales[:, g, w0 : w0 + n],
                        start=(c == first_chunk[s] and g == 0),
                        stop=(c == last_chunk[s] and g == CHUNK_PASSES - 1),
                    )
            if c == last_chunk[s] and g_first + g_count == CHUNK_PASSES:
                if stages[s]["out_col"] == 0:
                    finish_with_bias(sums_of[s], 0)
                else:
                    finish_complex(sums_of[s], products[0][2], stages[s]["out_col"])

        raw_of = {}
        for j in range(TILES_AHEAD):
            raw_of[j] = load(j)

        j = 0
        banks_done = 0
        copied = None
        before = None
        for c, (s, views) in enumerate(chunks):
            columns = len(views) * P
            codes = quantised_pool.tile([P, CHUNK_PASSES, columns], U32, tag="codes", align_bytes=64)
            scales = quantised_pool.tile([P, CHUNK_PASSES, columns], U8, tag="scales", align_bytes=64)
            run_banks = len(views) * RUN_PASSES // BANK_PASSES
            banks_in_chunk = 0

            for t in range(len(views)):
                if j + TILES_AHEAD < len(tile_views):
                    raw_of[j + TILES_AHEAD] = load(j + TILES_AHEAD)
                words = raw_of[j][:].bitcast(F32)
                j += 1
                for g0 in range(0, CHUNK_PASSES, BANK_PASSES):
                    bank = bank_pool.tile([P, BANK_F32], F32, tag="bank")
                    for b in range(BANK_PASSES * HALVES):
                        word0 = (g0 * HALVES + b) * P
                        nc.tensor.transpose(bank[:, b * P : (b + 1) * P], words[:, word0 : word0 + P], identity[:])
                    grouped = grouped_pool.tile([P, BANK_PASSES * K_PASS], BF16, tag="grouped", align_bytes=64)
                    copy_out = grouped[:].bitcast(F32).rearrange("p (i r u) -> p i r u", i=BANK_PASSES, u=HALVES)
                    copy_in = bank[:].rearrange("p (i u r) -> p i r u", i=BANK_PASSES, u=HALVES)
                    if banks_done % VECTOR_COPY_EVERY == VECTOR_COPY_EVERY - 1:
                        nc.vector.tensor_copy(out=copy_out, in_=copy_in)
                    else:
                        nc.scalar.copy(out=copy_out, in_=copy_in)
                    banks_done += 1
                    if copied is not None:
                        quantise(*copied)
                    copied = (grouped, codes, scales, g0, slice(t * P, (t + 1) * P))

                    banks_in_chunk += 1
                    if before is not None and banks_in_chunk % run_banks == 0:
                        multiply(*before, (banks_in_chunk // run_banks - 1) * RUN_PASSES, RUN_PASSES)
            before = (c, codes, scales)

        quantise(*copied)
        multiply(*before, 0, CHUNK_PASSES)
